import numpy as np
import ml_dtypes


def mxq(x, axis, fmt="e4m3"):
    dtype, down = {"e4m3": (ml_dtypes.float8_e4m3fn, 7), "e5m2": (ml_dtypes.float8_e5m2, 14)}[fmt]
    v = np.moveaxis(np.asarray(x, np.float32).astype(ml_dtypes.bfloat16).astype(np.float64), axis, -1)
    blocks = v.reshape(v.shape[:-1] + (-1, 32))
    amax = np.abs(blocks).max(-1, keepdims=True)
    byte = np.maximum(np.where(amax > 0, np.frexp(amax)[1] - 1 + 127, 0) - down, 1)
    scale = np.exp2(byte - 127.0)
    codes = (blocks / scale).astype(np.float32).astype(dtype).astype(np.float64)
    return np.moveaxis((codes * scale).reshape(v.shape), -1, axis)


WIDE = False


def mx_kscale(k):
    if not WIDE:
        return np.ones(k)
    levels = np.array([10, -10, 5, -5, 0])
    if k % 512:
        return np.exp2(np.random.permutation(np.resize(levels, k // 32))).repeat(32)
    a = np.empty((k // 512, 16))
    for p in range(k // 512):
        a[p, :8] = np.random.permutation(np.resize(levels, 8))
        for g in range(8):
            far = levels[np.abs(levels - a[p, g]) >= 10]
            a[p, g + 8] = far[np.random.randint(len(far))]
    return np.exp2(a.ravel()).repeat(32)


BF16 = ml_dtypes.bfloat16


def bf(x):
    return np.asarray(x, np.float32).astype(BF16)


def f64(x):
    return np.asarray(x).astype(np.float64)


B, S, H, NH, NKV, HD, W = 1, 1024, 1536, 12, 4, 128, 512
T = B * S
NQ = NH * HD
NK = NKV * HD
HALF = HD // 2
THETA = 10000.0


def rope(x, cos, sin):
    x1, x2 = x[..., :HALF], x[..., HALF:]
    c, s = cos[:, None, :], sin[:, None, :]
    return np.concatenate([x1 * c - x2 * s, x2 * c + x1 * s], axis=-1)


def draw0():
    s = mx_kscale(H)
    pos = np.tile(np.arange(S), B)
    inv_freq = 1.0 / THETA ** (np.arange(0, HD, 2) / HD)
    angles = pos[:, None] * inv_freq[None, :]
    return {"hidden_states": bf(np.random.standard_normal((T, H)) * s),
            "cos": bf(np.cos(angles)), "sin": bf(np.sin(angles)),
            "qkv_w": bf(np.random.standard_normal((NQ + 2 * NK, H)) * 1.25 / np.sqrt(H) / s),
            "qkv_b": bf(np.random.standard_normal(NQ + 2 * NK) * 0.5)}


def core(hidden_states, cos, sin, qkv_w, qkv_b):
    qkv = (mxq(f64(hidden_states), 1, "e4m3") @ mxq(f64(qkv_w), 1, "e4m3").T) + f64(qkv_b)
    q = qkv[:, :NQ].reshape(T, NH, HD)
    k = qkv[:, NQ:NQ + NK].reshape(T, NKV, HD)
    v = qkv[:, NQ + NK:].reshape(T, NKV, HD)
    return rope(q, f64(cos), f64(sin)), rope(k, f64(cos), f64(sin)), v


def e4m3fn_bytes(y):
    return np.clip(np.asarray(y, np.float64), -448.0, 448.0).astype(np.float32).astype(ml_dtypes.float8_e4m3fn).view(np.uint8)


def e4m3fn_values(b):
    return np.asarray(b, np.uint8).view(ml_dtypes.float8_e4m3fn).astype(np.float64)


def setup_inputs():
    d = draw0()
    x0 = np.asarray(d['qkv_w']).astype(np.float64)
    s = (np.max(np.abs(x0), axis=(0,), keepdims=True) / 448.0).astype(np.float32)
    out = {}
    for k, v in d.items():
        if k == 'qkv_w':
            out['qkv_w_bytes'] = e4m3fn_bytes(x0 / s.astype(np.float64))
            out['qkv_w_scale'] = s
        else:
            out[k] = v
    return out


def reference(hidden_states, cos, sin, qkv_w_bytes, qkv_w_scale, qkv_b):
    return core(hidden_states, cos, sin, e4m3fn_values(qkv_w_bytes) * qkv_w_scale.astype(np.float64), qkv_b)

@@ -1,0 +1,342 @@
+from contextlib import ExitStack
+
+import concourse.masks as masks
+import concourse.mybir as mybir
+
+F32 = mybir.dt.float32
+BF16 = mybir.dt.bfloat16
+U32 = mybir.dt.uint32
+U8 = mybir.dt.uint8
+FP8 = mybir.dt.float8_e4m3fn
+FP8X4 = mybir.dt.float8_e4m3fn_x4
+ALU = mybir.AluOpType
+ACT = mybir.ActivationFunctionType
+
+P = 128
+T = 1024
+K = 1536
+HEADS = 20
+Q_HEADS = 12
+ROPE_HEADS = 16
+HALF = 64
+K_PASS = 512
+PASSES = K // K_PASS
+WORDS = K_PASS // 2
+TOK_TILES = T // P
+N_TOK = 512
+TOK_HALVES = T // N_TOK
+BLOCKS = N_TOK // P
+PAIRS = HEADS // 2
+
+PAIR_ORDER = [8, 9, 0, 1, 2, 3, 4, 5, 6, 7]
+LAG = 3
+SORT_LAG = 3
+FIRST_SORTED = 4
+
+TW_BUFS = 3
+OT_BUFS = 2
+ACC_BUFS = 3
+
+FLOPS = 2 * T * K * HEADS * P
+
+
+def tile_flashqwen2attention_pa_kernel(
+    tc, hidden_states, cos, sin, qkv_w_bytes, qkv_w_scale, qkv_b, out_0, out_1, out_2
+):
+    nc = tc.nc
+
+    with ExitStack() as ctx:
+        const = ctx.enter_context(tc.tile_pool(name="const", bufs=1))
+        work = ctx.enter_context(tc.tile_pool(name="work", bufs=2))
+        psum = ctx.enter_context(tc.psum_pool(name="psum", bufs=2))
+        ctx.enter_context(tc.manual_schedule())
+
+        bank_bufs = {"tw": TW_BUFS, "ot": OT_BUFS, "acc": ACC_BUFS}
+
+        w_view = qkv_w_bytes.rearrange("(h p) k -> p h k", p=P)
+        hid_view = hidden_states.rearrange("(a p) k -> p a k", p=P)
+        w_bytes = {}
+        hid = {}
+
+        def load_w(i):
+            pair = PAIR_ORDER[i]
+            t = const.tile([P, 2, K], U8, name="w_bytes_%d" % i)
+            nc.sync.dma_start(out=t[:], in_=w_view[:, 2 * pair : 2 * pair + 2, :])
+            w_bytes[i] = t
+
+        def load_hid(a):
+            t = const.tile([P, K], BF16, name="hid_%d" % a)
+            nc.sync.dma_start(out=t[:], in_=hid_view[:, a, :])
+            hid[a] = t
+
+        s_rows = const.tile([P, P], F32, name="s_rows")
+        nc.gpsimd.memset(s_rows[:], 0.0)
+        nc.sync.dma_start(out=s_rows[0 : K // P, :], in_=qkv_w_scale.rearrange("o (c p) -> (o c) p", p=P))
+        b_rows = const.tile([P, P], BF16, name="b_rows")
+        nc.gpsimd.memset(b_rows[:], 0.0)
+        load_w(0)
+        nc.sync.dma_start(out=b_rows[0:HEADS, :], in_=qkv_b.rearrange("(h p) -> h p", p=P))
+        for a in range(0, 4):
+            load_hid(a)
+        load_w(1)
+        for a in range(4, 8):
+            load_hid(a)
+        load_w(2)
+        load_w(3)
+        cs_rows = const.tile([P, 2, TOK_TILES, P], BF16, name="cs_rows")
+        for which, table in enumerate((cos, sin)):
+            for half in range(2):
+                nc.sync.dma_start(
+                    out=cs_rows[:, which, :, half * HALF : (half + 1) * HALF],
+                    in_=table.rearrange("(a p) j -> p a j", p=P),
+                )
+        for i in range(4, PAIRS):
+            load_w(i)
+
+        ident = const.tile([P, P], F32, name="ident")
+        masks.make_identity(nc, ident[:])
+        ident_bf = const.tile([P, P], BF16, name="ident_bf")
+        masks.make_identity(nc, ident_bf[:])
+        swap = const.tile([P, P], F32, name="swap")
+        nc.vector.tensor_copy(out=swap[:, 0:HALF], in_=ident[:, HALF:P])
+        nc.vector.tensor_copy(out=swap[:, HALF:P], in_=ident[:, 0:HALF])
+        sgn = const.tile([P, 1], F32, name="sgn")
+        nc.vector.memset(sgn[0:HALF, :], 1.0)
+        nc.vector.memset(sgn[HALF:P, :], -1.0)
+        warm = const.tile([P, 1], F32, name="warm")
+        nc.scalar.activation(out=warm[:], in_=sgn[:], func=ACT.Identity)
+
+        scl_col = const.tile([P, K // P], F32, name="scl_col")
+        scl = const.tile([P, K], F32, name="scl")
+        bias_col = const.tile([P, HEADS], F32, name="bias_col")
+        cs_t = const.tile([P, 2, T], BF16, name="cs_t")
+
+        w_codes = const.tile([P, PASSES, HEADS * P], U32, name="w_codes", align_bytes=64)
+        w_scales = const.tile([P, PASSES, HEADS * P], U8, name="w_scales", align_bytes=64)
+        h_codes = const.tile([P, PASSES, T], U32, name="h_codes", align_bytes=64)
+        h_scales = const.tile([P, PASSES, T], U8, name="h_scales", align_bytes=64)
+
+        wide = {}
+        is_sorted = {}
+        grouped = {}
+
+        def widen(i, a, lo, hi):
+            if lo == 0:
+                wb = work.tile([P, K], BF16, tag="wb", name="wb", bufs=6)
+                wide[(i, a)] = wb
+            nc.vector.tensor_tensor(
+                out=wide[(i, a)][:, lo:hi], in0=w_bytes[i][:, a, lo:hi].bitcast(FP8), in1=scl[:, lo:hi],
+                op=ALU.mult,
+            )
+
+        def sort_words(i, a):
+            ws = work.tile([P, K], BF16, tag="ws", name="ws", bufs=6)
+            nc.scalar.copy(
+                out=ws[:].bitcast(F32).rearrange("p (g u w) -> p g u w", g=PASSES, u=2),
+                in_=wide[(i, a)][:].bitcast(F32).rearrange("p (g w u) -> p g u w", g=PASSES, u=2),
+            )
+            wide[(i, a)] = ws
+            is_sorted[(i, a)] = True
+
+        def turn(key, tag):
+            kind, i, g = key
+            rows_pair = (wide[(i, 0)], wide[(i, 1)]) if kind == "w" else (hid[2 * i], hid[2 * i + 1])
+            tw = psum.tile([P, 2, 2, P], F32, tag=tag, name="tw", bufs=bank_bufs[tag])
+            for a, rows in enumerate(rows_pair):
+                words = rows[:].bitcast(F32)
+                for u in range(2):
+                    if kind == "w" and is_sorted.get((i, a), False):
+                        picked = words[:, WORDS * g + P * u : WORDS * g + P * (u + 1)]
+                    else:
+                        picked = words[:, WORDS * g + u : WORDS * (g + 1) : 2]
+                    nc.tensor.transpose(tw[:, a, u, :], picked, ident[:])
+            grp = work.tile([P, 2 * P * 4], BF16, tag="grp", name="grp", bufs=9, align_bytes=64)
+            nc.scalar.copy(
+                out=grp[:].bitcast(F32).rearrange("p (a r u) -> p a r u", a=2, u=2),
+                in_=tw[:].rearrange("p a u r -> p a r u"),
+            )
+            grouped[key] = grp
+
+        def quantize(key):
+            kind, i, g = key
+            codes, scales = (w_codes, w_scales) if kind == "w" else (h_codes, h_scales)
+            cols = slice(2 * i * P, 2 * (i + 1) * P)
+            nc.vector.quantize_mx(
+                out=codes[:, g, cols].bitcast(FP8X4), scales=scales[:, g, cols], in_=grouped[key][:]
+            )
+
+        acc = {}
+        terms = {}
+        staged = {}
+
+        def multiply(unit):
+            i, th, a = unit
+            cols = slice((2 * i + a) * P, (2 * i + a + 1) * P)
+            toks = slice(th * N_TOK, (th + 1) * N_TOK)
+            bank = psum.tile([P, N_TOK], F32, tag="acc", name="acc", bufs=ACC_BUFS)
+            for g in range(PASSES):
+                nc.tensor.matmul_mx(
+                    out=bank[:],
+                    lhsT=w_codes[:, g, cols].bitcast(FP8X4),
+                    lhsT_scale=w_scales[:, g, cols],
+                    rhs=h_codes[:, g, toks].bitcast(FP8X4),
+                    rhs_scale=h_scales[:, g, toks],
+                    start=(g == 0),
+                    stop=(g == PASSES - 1),
+                )
+            acc[unit] = bank
+
+        def rotate(unit):
+            i, th, a = unit
+            head = 2 * PAIR_ORDER[i] + a
+            bank = acc[unit]
+            uv = work.tile([P, 2, N_TOK], F32, tag="uv", name="uv", bufs=6)
+            if head < ROPE_HEADS:
+                nc.vector.scalar_tensor_tensor(
+                    out=uv[:],
+                    in0=bank[:].unsqueeze(1).to_broadcast([P, 2, N_TOK]),
+                    scalar=bias_col[:, head : head + 1],
+                    in1=cs_t[:, :, th * N_TOK : (th + 1) * N_TOK],
+                    op0=ALU.add,
+                    op1=ALU.mult,
+                )
+            else:
+                nc.scalar.activation(
+                    out=uv[:, 0, :], in_=bank[:], func=ACT.Identity, bias=bias_col[:, head : head + 1]
+                )
+            terms[unit] = uv
+
+        def finish(unit):
+            i, th, a = unit
+            head0 = 2 * PAIR_ORDER[i]
+            if a == 0:
+                stg = work.tile([P, BLOCKS, 2 * P], F32, tag="stg", name="stg", bufs=3)
+                staged[(i, th)] = stg
+            stg = staged[(i, th)]
+            uv = terms[unit]
+            ot = psum.tile([P, BLOCKS, P], F32, tag="ot", name="ot", bufs=OT_BUFS)
+            for b in range(BLOCKS):
+                cols = slice(b * P, (b + 1) * P)
+                if head0 < ROPE_HEADS:
+                    nc.tensor.matmul(
+                        ot[:, b, :], lhsT=uv[:, 0, cols], rhs=ident[:], is_transpose=True, start=True, stop=False
+                    )
+                    nc.tensor.matmul(
+                        ot[:, b, :], lhsT=uv[:, 1, cols], rhs=swap[:], is_transpose=True, start=False, stop=True
+                    )
+                else:
+                    nc.tensor.transpose(ot[:, b, :], uv[:, 0, cols], ident[:])
+            nc.scalar.copy(out=stg[:, :, a * P : (a + 1) * P], in_=ot[:])
+            at_end = i == PAIRS - 1 and th == TOK_HALVES - 1
+            if a == 1 or at_end:
+                lo = a * P if at_end else 0
+                if head0 < Q_HEADS:
+                    dst, col = out_0, head0 * P
+                elif head0 < ROPE_HEADS:
+                    dst, col = out_1, (head0 - Q_HEADS) * P
+                else:
+                    dst, col = out_2, (head0 - ROPE_HEADS) * P
+                nc.sync.dma_start(
+                    out=dst.rearrange("(b p) h d -> p b (h d)", p=P)[
+                        :, th * BLOCKS : (th + 1) * BLOCKS, col + lo : col + (a + 1) * P
+                    ],
+                    in_=stg[:, :, lo : (a + 1) * P],
+                )
+
+        def bias_table():
+            bt = psum.tile([P, P], BF16, tag="tw", name="bt", bufs=TW_BUFS)
+            nc.tensor.transpose(bt[:], b_rows[:], ident_bf[:])
+            nc.vector.tensor_copy(out=bias_col[:], in_=bt[:, 0:HEADS])
+
+        def scale_columns():
+            sc = psum.tile([P, P], F32, tag="tw", name="sc", bufs=TW_BUFS)
+            nc.tensor.transpose(sc[:], s_rows[:], ident[:])
+            nc.vector.tensor_copy(out=scl_col[:], in_=sc[:, 0 : K // P])
+
+        def spread_scales(b):
+            st = psum.tile([P, BLOCKS, P], F32, tag="tw", name="st", bufs=TW_BUFS)
+            for c in range(BLOCKS):
+                col = BLOCKS * b + c
+                nc.tensor.transpose(st[:, c, :], scl_col[:, col : col + 1].to_broadcast([P, P]), ident[:])
+            nc.vector.tensor_copy(
+                out=scl[:, b * K_PASS : (b + 1) * K_PASS], in_=st[:].rearrange("p c n -> p (c n)")
+            )
+
+        def angle_tables():
+            for which in range(2):
+                ct = psum.tile([P, TOK_TILES, P], BF16, tag="tw", name="ct", bufs=TW_BUFS)
+                for a in range(TOK_TILES):
+                    nc.tensor.transpose(ct[:, a, :], cs_rows[:, which, a, :], ident_bf[:])
+                if which == 0:
+                    nc.scalar.copy(out=cs_t[:, 0, :], in_=ct[:].rearrange("p a t -> p (a t)"))
+                else:
+                    nc.scalar.activation(
+                        out=cs_t[:, 1, :], in_=ct[:].rearrange("p a t -> p (a t)"), func=ACT.Copy,
+                        scale=sgn[:, 0:1],
+                    )
+
+        scale_columns()
+        for g in range(PASSES):
+            spread_scales(g)
+            for a in range(2):
+                widen(0, a, g * K_PASS, (g + 1) * K_PASS)
+        head_keys = [("h", 0, g) for g in range(PASSES)]
+        head_keys += [("w", 0, g) for g in range(PASSES)]
+        head_keys += [("h", 1, g) for g in range(PASSES)]
+        head_tags = ["ot", "ot", "acc", "acc", "acc", "tw", "tw", "tw", "ot"]
+        for key, tag in zip(head_keys, head_tags):
+            turn(key, tag)
+        for key in head_keys:
+            quantize(key)
+        bias_table()
+
+        units = [(i, th, a) for i in range(PAIRS) for th in range(TOK_HALVES) for a in range(2)]
+        banks = [("h", 2, g) for g in range(PASSES)] + [("h", 3, g) for g in range(PASSES)]
+        banks += [("w", 1, g) for g in range(PASSES)] + ["tables"]
+        banks += [("w", i, g) for i in range(2, PAIRS) for g in range(PASSES)]
+        heads_to_widen = [(i, a) for i in range(1, PAIRS) for a in range(2)]
+
+        def banks_in_step(s):
+            if s < 3:
+                return (6, 3, 1)[s]
+            return 1 if s % 4 != 2 else 0
+
+        def widenings_in_step(s):
+            if s == 0:
+                return 2
+            if s < 8:
+                return 1
+            return 1 if (s - 8) % 5 in (0, 2) else 0
+
+        emptied = []
+        widened = []
+        next_head = 0
+        next_bank = 0
+        for s in range(len(units) + LAG):
+            for key in emptied:
+                quantize(key)
+            emptied = []
+            if s < len(units):
+                multiply(units[s])
+                rotate(units[s])
+            for i, a in widened[s - SORT_LAG] if s >= SORT_LAG else []:
+                sort_words(i, a)
+            widened.append([])
+            for n in range(widenings_in_step(s)):
+                if next_head < len(heads_to_widen):
+                    i, a = heads_to_widen[next_head]
+                    next_head += 1
+                    widen(i, a, 0, K)
+                    if i >= FIRST_SORTED:
+                        widened[s].append((i, a))
+            if s >= LAG:
+                finish(units[s - LAG])
+            for n in range(banks_in_step(s)):
+                if next_bank < len(banks):
+                    key = banks[next_bank]
+                    next_bank += 1
+                    if key == "tables":
+                        angle_tables()
+                    else:
+                        turn(key, "tw")
+                        emptied.append(key)

@@ -32,6 +32,10 @@ PAIR_ORDER = [8, 9, 0, 1, 2, 3, 4, 5, 6, 7]
 LAG = 3
 SORT_LAG = 3
 FIRST_SORTED = 4
+GP_FIRST = 5
+GP_START = 8
+GP_MARGIN = 2
+VEC_AHEAD = 6
 
 TW_BUFS = 3
 OT_BUFS = 2
@@ -137,6 +141,44 @@ def tile_flashqwen2attention_pa_kernel(
             )
             wide[(i, a)] = ws
             is_sorted[(i, a)] = True
+
+        raw = {}
+
+        def late_tiles(i, a):
+            if (i, a) not in raw:
+                rw = work.tile([P, K], BF16, tag="wb", name="rw", bufs=6)
+                raw[(i, a)] = rw
+                ws = work.tile([P, K], BF16, tag="ws", name="ws", bufs=6)
+                wide[(i, a)] = ws
+                is_sorted[(i, a)] = True
+
+        def cast_part(i, a, g):
+            late_tiles(i, a)
+            cols = slice(g * K_PASS, (g + 1) * K_PASS)
+            nc.scalar.copy(out=raw[(i, a)][:, cols], in_=w_bytes[i][:, a, cols].bitcast(FP8))
+
+        def scale_part(i, a, g):
+            cols = slice(g * K_PASS, (g + 1) * K_PASS)
+            nc.gpsimd.tensor_tensor(
+                out=wide[(i, a)][:, cols].rearrange("p (u w e) -> p u w e", u=2, e=2),
+                in0=raw[(i, a)][:, cols].rearrange("p (w u e) -> p u w e", u=2, e=2),
+                in1=scl[:, cols].rearrange("p (w u e) -> p u w e", u=2, e=2),
+                op=ALU.mult,
+            )
+
+        def widen_part(i, a, g):
+            late_tiles(i, a)
+            cols = slice(g * K_PASS, (g + 1) * K_PASS)
+            nc.vector.tensor_tensor(
+                out=raw[(i, a)][:, cols], in0=w_bytes[i][:, a, cols].bitcast(FP8), in1=scl[:, cols], op=ALU.mult
+            )
+
+        def sort_part(i, a, g):
+            cols = slice(g * K_PASS, (g + 1) * K_PASS)
+            nc.scalar.copy(
+                out=wide[(i, a)][:, cols].bitcast(F32).rearrange("p (u w) -> p u w", u=2),
+                in_=raw[(i, a)][:, cols].bitcast(F32).rearrange("p (w u) -> p u w", u=2),
+            )
 
         def turn(key, tag):
             kind, i, g = key
@@ -294,7 +336,7 @@ def tile_flashqwen2attention_pa_kernel(
         banks = [("h", 2, g) for g in range(PASSES)] + [("h", 3, g) for g in range(PASSES)]
         banks += [("w", 1, g) for g in range(PASSES)] + ["tables"]
         banks += [("w", i, g) for i in range(2, PAIRS) for g in range(PASSES)]
-        heads_to_widen = [(i, a) for i in range(1, PAIRS) for a in range(2)]
+        heads_to_widen = [(i, a) for i in range(1, GP_FIRST) for a in range(2)]
 
         def banks_in_step(s):
             if s < 3:
@@ -307,6 +349,29 @@ def tile_flashqwen2attention_pa_kernel(
             if s < 8:
                 return 1
             return 1 if (s - 8) % 5 in (0, 2) else 0
+
+        turn_step = {}
+        counted = 0
+        for s in range(len(units) + LAG):
+            for n in range(banks_in_step(s)):
+                if counted < len(banks):
+                    turn_step[banks[counted]] = s
+                    counted += 1
+        gp_parts = {}
+        vec_parts = {}
+        sort_parts = {}
+        gp_step = GP_START
+        for i in range(GP_FIRST, PAIRS):
+            for g in range(PASSES):
+                due = turn_step[("w", i, g)]
+                if gp_step + 1 + GP_MARGIN <= due:
+                    gp_parts[gp_step] = (i, 0, g)
+                    gp_parts[gp_step + 1] = (i, 1, g)
+                    gp_step += 2
+                else:
+                    for a in range(2):
+                        vec_parts[due - VEC_AHEAD + a] = (i, a, g)
+                        sort_parts[due - VEC_AHEAD + a + SORT_LAG] = (i, a, g)
 
         emptied = []
         widened = []
@@ -321,6 +386,16 @@ def tile_flashqwen2attention_pa_kernel(
                 rotate(units[s])
             for i, a in widened[s - SORT_LAG] if s >= SORT_LAG else []:
                 sort_words(i, a)
+            if s in gp_parts:
+                i, a, g = gp_parts[s]
+                cast_part(i, a, g)
+                scale_part(i, a, g)
+            if s in sort_parts:
+                i, a, g = sort_parts[s]
+                sort_part(i, a, g)
+            if s in vec_parts:
+                i, a, g = vec_parts[s]
+                widen_part(i, a, g)
             widened.append([])
             for n in range(widenings_in_step(s)):
                 if next_head < len(heads_to_widen):

@@ -30,6 +30,7 @@ PAIRS = HEADS // 2
 
 PAIR_ORDER = [8, 9, 0, 1, 2, 3, 4, 5, 6, 7]
 LAG = 3
+GROUP = 2
 SORT_LAG = 3
 FIRST_SORTED = 4
 GP_FIRST = 5
@@ -377,41 +378,47 @@ def tile_flashqwen2attention_pa_kernel(
         widened = []
         next_head = 0
         next_bank = 0
-        for s in range(len(units) + LAG):
+        steps = len(units) + LAG
+        for s0 in range(0, steps + (-steps) % GROUP, GROUP):
+            group = range(s0, s0 + GROUP)
             for key in emptied:
                 quantize(key)
             emptied = []
-            if s < len(units):
-                multiply(units[s])
-                rotate(units[s])
-            for i, a in widened[s - SORT_LAG] if s >= SORT_LAG else []:
-                sort_words(i, a)
-            if s in gp_parts:
-                i, a, g = gp_parts[s]
-                cast_part(i, a, g)
-                scale_part(i, a, g)
-            if s in sort_parts:
-                i, a, g = sort_parts[s]
-                sort_part(i, a, g)
-            if s in vec_parts:
-                i, a, g = vec_parts[s]
-                widen_part(i, a, g)
-            widened.append([])
-            for n in range(widenings_in_step(s)):
-                if next_head < len(heads_to_widen):
-                    i, a = heads_to_widen[next_head]
-                    next_head += 1
-                    widen(i, a, 0, K)
-                    if i >= FIRST_SORTED:
-                        widened[s].append((i, a))
-            if s >= LAG:
-                finish(units[s - LAG])
-            for n in range(banks_in_step(s)):
-                if next_bank < len(banks):
-                    key = banks[next_bank]
-                    next_bank += 1
-                    if key == "tables":
-                        angle_tables()
-                    else:
-                        turn(key, "tw")
-                        emptied.append(key)
+            for s in group:
+                if s < len(units):
+                    multiply(units[s])
+                    rotate(units[s])
+            for s in group:
+                for i, a in widened[s - SORT_LAG] if s >= SORT_LAG else []:
+                    sort_words(i, a)
+                if s in gp_parts:
+                    i, a, g = gp_parts[s]
+                    cast_part(i, a, g)
+                    scale_part(i, a, g)
+                if s in sort_parts:
+                    i, a, g = sort_parts[s]
+                    sort_part(i, a, g)
+                if s in vec_parts:
+                    i, a, g = vec_parts[s]
+                    widen_part(i, a, g)
+                widened.append([])
+                for n in range(widenings_in_step(s)):
+                    if next_head < len(heads_to_widen):
+                        i, a = heads_to_widen[next_head]
+                        next_head += 1
+                        widen(i, a, 0, K)
+                        if i >= FIRST_SORTED:
+                            widened[s].append((i, a))
+            for s in group:
+                if LAG <= s < len(units) + LAG:
+                    finish(units[s - LAG])
+            for s in group:
+                for n in range(banks_in_step(s)):
+                    if next_bank < len(banks):
+                        key = banks[next_bank]
+                        next_bank += 1
+                        if key == "tables":
+                            angle_tables()
+                        else:
+                            turn(key, "tw")
+                            emptied.append(key)

@@ -29,18 +29,25 @@ BLOCKS = N_TOK // P
 PAIRS = HEADS // 2
 
 PAIR_ORDER = [8, 9, 0, 1, 2, 3, 4, 5, 6, 7]
-LAG = 3
+LAG = 4
+BIG_FROM = 8
+VEC_EXIT_FROM = 4
+VEC_EXIT_G = 2
+PART_SORT_LAG = 4
+BIG = 4
+EARLY = 12
+SKIP = 0
 GROUP = 2
 SORT_LAG = 3
 FIRST_SORTED = 4
 GP_FIRST = 5
 GP_START = 8
 GP_MARGIN = 2
-VEC_AHEAD = 6
+VEC_AHEAD = 8
 
-TW_BUFS = 3
-OT_BUFS = 2
-ACC_BUFS = 3
+BANKS = 8
+UV_BUFS = 8
+STG_BUFS = 4
 
 FLOPS = 2 * T * K * HEADS * P
 
@@ -56,7 +63,6 @@ def tile_flashqwen2attention_pa_kernel(
         psum = ctx.enter_context(tc.psum_pool(name="psum", bufs=2))
         ctx.enter_context(tc.manual_schedule())
 
-        bank_bufs = {"tw": TW_BUFS, "ot": OT_BUFS, "acc": ACC_BUFS}
 
         w_view = qkv_w_bytes.rearrange("(h p) k -> p h k", p=P)
         hid_view = hidden_states.rearrange("(a p) k -> p a k", p=P)
@@ -184,7 +190,7 @@ def tile_flashqwen2attention_pa_kernel(
         def turn(key, tag):
             kind, i, g = key
             rows_pair = (wide[(i, 0)], wide[(i, 1)]) if kind == "w" else (hid[2 * i], hid[2 * i + 1])
-            tw = psum.tile([P, 2, 2, P], F32, tag=tag, name="tw", bufs=bank_bufs[tag])
+            tw = psum.tile([P, 2, 2, P], F32, tag="bank", name="tw", bufs=BANKS)
             for a, rows in enumerate(rows_pair):
                 words = rows[:].bitcast(F32)
                 for u in range(2):
@@ -194,10 +200,16 @@ def tile_flashqwen2attention_pa_kernel(
                         picked = words[:, WORDS * g + u : WORDS * (g + 1) : 2]
                     nc.tensor.transpose(tw[:, a, u, :], picked, ident[:])
             grp = work.tile([P, 2 * P * 4], BF16, tag="grp", name="grp", bufs=9, align_bytes=64)
-            nc.scalar.copy(
-                out=grp[:].bitcast(F32).rearrange("p (a r u) -> p a r u", a=2, u=2),
-                in_=tw[:].rearrange("p a u r -> p a r u"),
-            )
+            if kind == "w" and i >= VEC_EXIT_FROM and g >= VEC_EXIT_G:
+                nc.vector.tensor_copy(
+                    out=grp[:].bitcast(F32).rearrange("p (a r u) -> p a r u", a=2, u=2),
+                    in_=tw[:].rearrange("p a u r -> p a r u"),
+                )
+            else:
+                nc.scalar.copy(
+                    out=grp[:].bitcast(F32).rearrange("p (a r u) -> p a r u", a=2, u=2),
+                    in_=tw[:].rearrange("p a u r -> p a r u"),
+                )
             grouped[key] = grp
 
         def quantize(key):
@@ -216,7 +228,7 @@ def tile_flashqwen2attention_pa_kernel(
             i, th, a = unit
             cols = slice((2 * i + a) * P, (2 * i + a + 1) * P)
             toks = slice(th * N_TOK, (th + 1) * N_TOK)
-            bank = psum.tile([P, N_TOK], F32, tag="acc", name="acc", bufs=ACC_BUFS)
+            bank = psum.tile([P, N_TOK], F32, tag="bank", name="acc", bufs=BANKS)
             for g in range(PASSES):
                 nc.tensor.matmul_mx(
                     out=bank[:],
@@ -233,7 +245,7 @@ def tile_flashqwen2attention_pa_kernel(
             i, th, a = unit
             head = 2 * PAIR_ORDER[i] + a
             bank = acc[unit]
-            uv = work.tile([P, 2, N_TOK], F32, tag="uv", name="uv", bufs=6)
+            uv = work.tile([P, 2, N_TOK], F32, tag="uv", name="uv", bufs=UV_BUFS)
             if head < ROPE_HEADS:
                 nc.vector.scalar_tensor_tensor(
                     out=uv[:],
@@ -253,11 +265,11 @@ def tile_flashqwen2attention_pa_kernel(
             i, th, a = unit
             head0 = 2 * PAIR_ORDER[i]
             if a == 0:
-                stg = work.tile([P, BLOCKS, 2 * P], F32, tag="stg", name="stg", bufs=3)
+                stg = work.tile([P, BLOCKS, 2 * P], F32, tag="stg", name="stg", bufs=STG_BUFS)
                 staged[(i, th)] = stg
             stg = staged[(i, th)]
             uv = terms[unit]
-            ot = psum.tile([P, BLOCKS, P], F32, tag="ot", name="ot", bufs=OT_BUFS)
+            ot = psum.tile([P, BLOCKS, P], F32, tag="bank", name="ot", bufs=BANKS)
             for b in range(BLOCKS):
                 cols = slice(b * P, (b + 1) * P)
                 if head0 < ROPE_HEADS:
@@ -287,17 +299,17 @@ def tile_flashqwen2attention_pa_kernel(
                 )
 
         def bias_table():
-            bt = psum.tile([P, P], BF16, tag="tw", name="bt", bufs=TW_BUFS)
+            bt = psum.tile([P, P], BF16, tag="bank", name="bt", bufs=BANKS)
             nc.tensor.transpose(bt[:], b_rows[:], ident_bf[:])
             nc.vector.tensor_copy(out=bias_col[:], in_=bt[:, 0:HEADS])
 
         def scale_columns():
-            sc = psum.tile([P, P], F32, tag="tw", name="sc", bufs=TW_BUFS)
+            sc = psum.tile([P, P], F32, tag="bank", name="sc", bufs=BANKS)
             nc.tensor.transpose(sc[:], s_rows[:], ident[:])
             nc.vector.tensor_copy(out=scl_col[:], in_=sc[:, 0 : K // P])
 
         def spread_scales(b):
-            st = psum.tile([P, BLOCKS, P], F32, tag="tw", name="st", bufs=TW_BUFS)
+            st = psum.tile([P, BLOCKS, P], F32, tag="bank", name="st", bufs=BANKS)
             for c in range(BLOCKS):
                 col = BLOCKS * b + c
                 nc.tensor.transpose(st[:, c, :], scl_col[:, col : col + 1].to_broadcast([P, P]), ident[:])
@@ -307,7 +319,7 @@ def tile_flashqwen2attention_pa_kernel(
 
         def angle_tables():
             for which in range(2):
-                ct = psum.tile([P, TOK_TILES, P], BF16, tag="tw", name="ct", bufs=TW_BUFS)
+                ct = psum.tile([P, TOK_TILES, P], BF16, tag="bank", name="ct", bufs=BANKS)
                 for a in range(TOK_TILES):
                     nc.tensor.transpose(ct[:, a, :], cs_rows[:, which, a, :], ident_bf[:])
                 if which == 0:
@@ -341,8 +353,10 @@ def tile_flashqwen2attention_pa_kernel(
 
         def banks_in_step(s):
             if s < 3:
-                return (6, 3, 1)[s]
-            return 1 if s % 4 != 2 else 0
+                return (6, 3, 2)[s]
+            if s < EARLY:
+                return 1
+            return 1 if s % 4 != SKIP else 0
 
         def widenings_in_step(s):
             if s == 0:
@@ -372,22 +386,27 @@ def tile_flashqwen2attention_pa_kernel(
                 else:
                     for a in range(2):
                         vec_parts[due - VEC_AHEAD + a] = (i, a, g)
-                        sort_parts[due - VEC_AHEAD + a + SORT_LAG] = (i, a, g)
+                        sort_parts[due - VEC_AHEAD + a + PART_SORT_LAG] = (i, a, g)
 
         emptied = []
         widened = []
         next_head = 0
         next_bank = 0
         steps = len(units) + LAG
-        for s0 in range(0, steps + (-steps) % GROUP, GROUP):
-            group = range(s0, s0 + GROUP)
-            for key in emptied:
-                quantize(key)
-            emptied = []
+        starts = list(range(0, BIG_FROM, GROUP)) + list(range(BIG_FROM, steps, BIG))
+        for s0, s1 in zip(starts, starts[1:] + [steps]):
+            group = range(s0, s1)
+            if s0 < BIG_FROM:
+                for key in emptied:
+                    quantize(key)
+                emptied = []
             for s in group:
                 if s < len(units):
                     multiply(units[s])
                     rotate(units[s])
+            for key in emptied:
+                quantize(key)
+            emptied = []
             for s in group:
                 for i, a in widened[s - SORT_LAG] if s >= SORT_LAG else []:
                     sort_words(i, a)

@@ -32,7 +32,7 @@ PAIR_ORDER = [8, 9, 0, 1, 2, 3, 4, 5, 6, 7]
 LAG = 4
 BIG_FROM = 8
 VEC_EXIT_FROM = 4
-VEC_EXIT_G = 2
+VEC_EXIT_G = 1
 PART_SORT_LAG = 4
 BIG = 4
 EARLY = 12

@@ -298,6 +298,40 @@ def tile_flashqwen2attention_pa_kernel(
                     in_=stg[:, :, lo : (a + 1) * P],
                 )
 
+        def finish_both(unit0, unit1):
+            i, th, a0 = unit0
+            head0 = 2 * PAIR_ORDER[i]
+            stg = work.tile([P, BLOCKS, 2 * P], F32, tag="stg", name="stg", bufs=STG_BUFS)
+            ots = []
+            for unit in (unit0, unit1):
+                ot = psum.tile([P, BLOCKS, P], F32, tag="bank", name="ot", bufs=BANKS)
+                ots.append(ot)
+            for b in range(BLOCKS):
+                cols = slice(b * P, (b + 1) * P)
+                for ot, unit in zip(ots, (unit0, unit1)):
+                    nc.tensor.matmul(
+                        ot[:, b, :], lhsT=terms[unit][:, 0, cols], rhs=ident[:], is_transpose=True, start=True, stop=False
+                    )
+                for ot, unit in zip(ots, (unit0, unit1)):
+                    nc.tensor.matmul(
+                        ot[:, b, :], lhsT=terms[unit][:, 1, cols], rhs=swap[:], is_transpose=True, start=False, stop=True
+                    )
+            if head0 < Q_HEADS:
+                dst, col = out_0, head0 * P
+            else:
+                dst, col = out_1, (head0 - Q_HEADS) * P
+            at_end = i == PAIRS - 1 and th == TOK_HALVES - 1
+            for a, ot in enumerate(ots):
+                nc.scalar.copy(out=stg[:, :, a * P : (a + 1) * P], in_=ot[:])
+                if a == 1 or at_end:
+                    lo = a * P if at_end else 0
+                    nc.sync.dma_start(
+                        out=dst.rearrange("(b p) h d -> p b (h d)", p=P)[
+                            :, th * BLOCKS : (th + 1) * BLOCKS, col + lo : col + (a + 1) * P
+                        ],
+                        in_=stg[:, :, lo : (a + 1) * P],
+                    )
+
         def bias_table():
             bt = psum.tile([P, P], BF16, tag="bank", name="bt", bufs=BANKS)
             nc.tensor.transpose(bt[:], b_rows[:], ident_bf[:])
@@ -430,7 +464,10 @@ def tile_flashqwen2attention_pa_kernel(
                             widened[s].append((i, a))
             for s in group:
                 if LAG <= s < len(units) + LAG:
-                    finish(units[s - LAG])
+                    if 2 * PAIR_ORDER[units[s - LAG][0]] >= ROPE_HEADS or s - LAG >= len(units) - 2:
+                        finish(units[s - LAG])
+                    elif units[s - LAG][2] == 0:
+                        finish_both(units[s - LAG], units[s - LAG + 1])
             for s in group:
                 for n in range(banks_in_step(s)):
                     if next_bank < len(banks):

@@ -27,27 +27,17 @@ N_TOK = 512
 TOK_HALVES = T // N_TOK
 BLOCKS = N_TOK // P
 PAIRS = HEADS // 2
+VALUE_PAIRS = 2
 
-PAIR_ORDER = [8, 9, 0, 1, 2, 3, 4, 5, 6, 7]
-LAG = 4
-BIG_FROM = 8
-VEC_EXIT_FROM = 4
-VEC_EXIT_G = 1
-PART_SORT_LAG = 4
-BIG = 4
-EARLY = 12
-SKIP = 0
-GROUP = 2
-SORT_LAG = 3
-FIRST_SORTED = 4
-GP_FIRST = 5
-GP_START = 8
-GP_MARGIN = 2
-VEC_AHEAD = 8
+PAIR_ORDER = [0, 1, 2, 3, 4, 5, 6, 7, 8, 9]
+ROPE_PAIRS = 8
 
 BANKS = 8
 UV_BUFS = 8
 STG_BUFS = 4
+RAW_BUFS = 10
+WS_BUFS = 20
+GRP_BUFS = 9
 
 FLOPS = 2 * T * K * HEADS * P
 
@@ -62,7 +52,6 @@ def tile_flashqwen2attention_pa_kernel(
         work = ctx.enter_context(tc.tile_pool(name="work", bufs=2))
         psum = ctx.enter_context(tc.psum_pool(name="psum", bufs=2))
         ctx.enter_context(tc.manual_schedule())
-
 
         w_view = qkv_w_bytes.rearrange("(h p) k -> p h k", p=P)
         hid_view = hidden_states.rearrange("(a p) k -> p a k", p=P)
@@ -85,15 +74,11 @@ def tile_flashqwen2attention_pa_kernel(
         nc.sync.dma_start(out=s_rows[0 : K // P, :], in_=qkv_w_scale.rearrange("o (c p) -> (o c) p", p=P))
         b_rows = const.tile([P, P], BF16, name="b_rows")
         nc.gpsimd.memset(b_rows[:], 0.0)
-        load_w(0)
         nc.sync.dma_start(out=b_rows[0:HEADS, :], in_=qkv_b.rearrange("(h p) -> h p", p=P))
+        load_w(0)
         for a in range(0, 4):
             load_hid(a)
         load_w(1)
-        for a in range(4, 8):
-            load_hid(a)
-        load_w(2)
-        load_w(3)
         cs_rows = const.tile([P, 2, TOK_TILES, P], BF16, name="cs_rows")
         for which, table in enumerate((cos, sin)):
             for half in range(2):
@@ -101,7 +86,10 @@ def tile_flashqwen2attention_pa_kernel(
                     out=cs_rows[:, which, :, half * HALF : (half + 1) * HALF],
                     in_=table.rearrange("(a p) j -> p a j", p=P),
                 )
-        for i in range(4, PAIRS):
+        load_w(2)
+        for a in range(4, 8):
+            load_hid(a)
+        for i in range(3, PAIRS):
             load_w(i)
 
         ident = const.tile([P, P], F32, name="ident")
@@ -120,6 +108,7 @@ def tile_flashqwen2attention_pa_kernel(
         scl_col = const.tile([P, K // P], F32, name="scl_col")
         scl = const.tile([P, K], F32, name="scl")
         bias_col = const.tile([P, HEADS], F32, name="bias_col")
+        bias_row = const.tile([P, VALUE_PAIRS * 2 * P], F32, name="bias_row")
         cs_t = const.tile([P, 2, T], BF16, name="cs_t")
 
         w_codes = const.tile([P, PASSES, HEADS * P], U32, name="w_codes", align_bytes=64)
@@ -127,80 +116,81 @@ def tile_flashqwen2attention_pa_kernel(
         h_codes = const.tile([P, PASSES, T], U32, name="h_codes", align_bytes=64)
         h_scales = const.tile([P, PASSES, T], U8, name="h_scales", align_bytes=64)
 
-        wide = {}
+        raw = {}
+        part = {}
         is_sorted = {}
         grouped = {}
 
-        def widen(i, a, lo, hi):
-            if lo == 0:
-                wb = work.tile([P, K], BF16, tag="wb", name="wb", bufs=6)
-                wide[(i, a)] = wb
+        def cols_of(g):
+            return slice(g * K_PASS, (g + 1) * K_PASS)
+
+        def widen_plain(i, a, g):
+            t = work.tile([P, K_PASS], BF16, tag="ws", name="ws", bufs=WS_BUFS)
             nc.vector.tensor_tensor(
-                out=wide[(i, a)][:, lo:hi], in0=w_bytes[i][:, a, lo:hi].bitcast(FP8), in1=scl[:, lo:hi],
-                op=ALU.mult,
+                out=t[:], in0=w_bytes[i][:, a, cols_of(g)].bitcast(FP8), in1=scl[:, cols_of(g)], op=ALU.mult
             )
-
-        def sort_words(i, a):
-            ws = work.tile([P, K], BF16, tag="ws", name="ws", bufs=6)
-            nc.scalar.copy(
-                out=ws[:].bitcast(F32).rearrange("p (g u w) -> p g u w", g=PASSES, u=2),
-                in_=wide[(i, a)][:].bitcast(F32).rearrange("p (g w u) -> p g u w", g=PASSES, u=2),
-            )
-            wide[(i, a)] = ws
-            is_sorted[(i, a)] = True
-
-        raw = {}
-
-        def late_tiles(i, a):
-            if (i, a) not in raw:
-                rw = work.tile([P, K], BF16, tag="wb", name="rw", bufs=6)
-                raw[(i, a)] = rw
-                ws = work.tile([P, K], BF16, tag="ws", name="ws", bufs=6)
-                wide[(i, a)] = ws
-                is_sorted[(i, a)] = True
-
-        def cast_part(i, a, g):
-            late_tiles(i, a)
-            cols = slice(g * K_PASS, (g + 1) * K_PASS)
-            nc.scalar.copy(out=raw[(i, a)][:, cols], in_=w_bytes[i][:, a, cols].bitcast(FP8))
-
-        def scale_part(i, a, g):
-            cols = slice(g * K_PASS, (g + 1) * K_PASS)
-            nc.gpsimd.tensor_tensor(
-                out=wide[(i, a)][:, cols].rearrange("p (u w e) -> p u w e", u=2, e=2),
-                in0=raw[(i, a)][:, cols].rearrange("p (w u e) -> p u w e", u=2, e=2),
-                in1=scl[:, cols].rearrange("p (w u e) -> p u w e", u=2, e=2),
-                op=ALU.mult,
-            )
+            part[(i, a, g)] = t
+            is_sorted[(i, a, g)] = False
 
         def widen_part(i, a, g):
-            late_tiles(i, a)
-            cols = slice(g * K_PASS, (g + 1) * K_PASS)
+            t = work.tile([P, K_PASS], BF16, tag="raw", name="raw", bufs=RAW_BUFS)
             nc.vector.tensor_tensor(
-                out=raw[(i, a)][:, cols], in0=w_bytes[i][:, a, cols].bitcast(FP8), in1=scl[:, cols], op=ALU.mult
+                out=t[:], in0=w_bytes[i][:, a, cols_of(g)].bitcast(FP8), in1=scl[:, cols_of(g)], op=ALU.mult
             )
+            raw[(i, a, g)] = t
 
         def sort_part(i, a, g):
-            cols = slice(g * K_PASS, (g + 1) * K_PASS)
+            t = work.tile([P, K_PASS], BF16, tag="ws", name="ws", bufs=WS_BUFS)
             nc.scalar.copy(
-                out=wide[(i, a)][:, cols].bitcast(F32).rearrange("p (u w) -> p u w", u=2),
-                in_=raw[(i, a)][:, cols].bitcast(F32).rearrange("p (w u) -> p u w", u=2),
+                out=t[:].bitcast(F32).rearrange("p (u w) -> p u w", u=2),
+                in_=raw[(i, a, g)][:].bitcast(F32).rearrange("p (w u) -> p u w", u=2),
             )
+            part[(i, a, g)] = t
+            is_sorted[(i, a, g)] = True
 
-        def turn(key, tag):
-            kind, i, g = key
-            rows_pair = (wide[(i, 0)], wide[(i, 1)]) if kind == "w" else (hid[2 * i], hid[2 * i + 1])
+        def cast_part(i, a, g):
+            t = work.tile([P, K_PASS], BF16, tag="raw", name="raw", bufs=RAW_BUFS)
+            nc.scalar.copy(out=t[:], in_=w_bytes[i][:, a, cols_of(g)].bitcast(FP8))
+            raw[(i, a, g)] = t
+
+        def scale_part(i, a, g):
+            t = work.tile([P, K_PASS], BF16, tag="ws", name="ws", bufs=WS_BUFS)
+            nc.gpsimd.tensor_tensor(
+                out=t[:].rearrange("p (u w e) -> p u w e", u=2, e=2),
+                in0=raw[(i, a, g)][:].rearrange("p (w u e) -> p u w e", u=2, e=2),
+                in1=scl[:, cols_of(g)].rearrange("p (w u e) -> p u w e", u=2, e=2),
+                op=ALU.mult,
+            )
+            part[(i, a, g)] = t
+            is_sorted[(i, a, g)] = True
+
+        turned = {}
+
+        def open_bank(key):
             tw = psum.tile([P, 2, 2, P], F32, tag="bank", name="tw", bufs=BANKS)
-            for a, rows in enumerate(rows_pair):
-                words = rows[:].bitcast(F32)
-                for u in range(2):
-                    if kind == "w" and is_sorted.get((i, a), False):
-                        picked = words[:, WORDS * g + P * u : WORDS * g + P * (u + 1)]
-                    else:
-                        picked = words[:, WORDS * g + u : WORDS * (g + 1) : 2]
-                    nc.tensor.transpose(tw[:, a, u, :], picked, ident[:])
-            grp = work.tile([P, 2 * P * 4], BF16, tag="grp", name="grp", bufs=9, align_bytes=64)
-            if kind == "w" and i >= VEC_EXIT_FROM and g >= VEC_EXIT_G:
+            turned[key] = tw
+
+        def turn_rows(key, a):
+            kind, i, g = key
+            for u in range(2):
+                if kind == "h":
+                    picked = hid[2 * i + a][:].bitcast(F32)[:, WORDS * g + u : WORDS * (g + 1) : 2]
+                elif is_sorted[(i, a, g)]:
+                    picked = part[(i, a, g)][:].bitcast(F32)[:, P * u : P * (u + 1)]
+                else:
+                    picked = part[(i, a, g)][:].bitcast(F32)[:, u:WORDS:2]
+                nc.tensor.transpose(turned[key][:, a, u, :], picked, ident[:])
+
+        def turn(key, on_vector=False):
+            open_bank(key)
+            for a in range(2):
+                turn_rows(key, a)
+            empty(key, on_vector)
+
+        def empty(key, on_vector=False):
+            tw = turned[key]
+            grp = work.tile([P, 2 * P * 4], BF16, tag="grp", name="grp", bufs=GRP_BUFS, align_bytes=64)
+            if on_vector:
                 nc.vector.tensor_copy(
                     out=grp[:].bitcast(F32).rearrange("p (a r u) -> p a r u", a=2, u=2),
                     in_=tw[:].rearrange("p a u r -> p a r u"),
@@ -222,7 +212,6 @@ def tile_flashqwen2attention_pa_kernel(
 
         acc = {}
         terms = {}
-        staged = {}
 
         def multiply(unit):
             i, th, a = unit
@@ -244,87 +233,44 @@ def tile_flashqwen2attention_pa_kernel(
         def rotate(unit):
             i, th, a = unit
             head = 2 * PAIR_ORDER[i] + a
-            bank = acc[unit]
             uv = work.tile([P, 2, N_TOK], F32, tag="uv", name="uv", bufs=UV_BUFS)
-            if head < ROPE_HEADS:
-                nc.vector.scalar_tensor_tensor(
-                    out=uv[:],
-                    in0=bank[:].unsqueeze(1).to_broadcast([P, 2, N_TOK]),
-                    scalar=bias_col[:, head : head + 1],
-                    in1=cs_t[:, :, th * N_TOK : (th + 1) * N_TOK],
-                    op0=ALU.add,
-                    op1=ALU.mult,
-                )
-            else:
-                nc.scalar.activation(
-                    out=uv[:, 0, :], in_=bank[:], func=ACT.Identity, bias=bias_col[:, head : head + 1]
-                )
+            nc.vector.scalar_tensor_tensor(
+                out=uv[:],
+                in0=acc[unit][:].unsqueeze(1).to_broadcast([P, 2, N_TOK]),
+                scalar=bias_col[:, head : head + 1],
+                in1=cs_t[:, :, th * N_TOK : (th + 1) * N_TOK],
+                op0=ALU.add,
+                op1=ALU.mult,
+            )
             terms[unit] = uv
 
-        def finish(unit):
-            i, th, a = unit
-            head0 = 2 * PAIR_ORDER[i]
-            if a == 0:
-                stg = work.tile([P, BLOCKS, 2 * P], F32, tag="stg", name="stg", bufs=STG_BUFS)
-                staged[(i, th)] = stg
-            stg = staged[(i, th)]
-            uv = terms[unit]
-            ot = psum.tile([P, BLOCKS, P], F32, tag="bank", name="ot", bufs=BANKS)
-            for b in range(BLOCKS):
-                cols = slice(b * P, (b + 1) * P)
-                if head0 < ROPE_HEADS:
-                    nc.tensor.matmul(
-                        ot[:, b, :], lhsT=uv[:, 0, cols], rhs=ident[:], is_transpose=True, start=True, stop=False
-                    )
-                    nc.tensor.matmul(
-                        ot[:, b, :], lhsT=uv[:, 1, cols], rhs=swap[:], is_transpose=True, start=False, stop=True
-                    )
-                else:
-                    nc.tensor.transpose(ot[:, b, :], uv[:, 0, cols], ident[:])
-            nc.scalar.copy(out=stg[:, :, a * P : (a + 1) * P], in_=ot[:])
-            at_end = i == PAIRS - 1 and th == TOK_HALVES - 1
-            if a == 1 or at_end:
-                lo = a * P if at_end else 0
-                if head0 < Q_HEADS:
-                    dst, col = out_0, head0 * P
-                elif head0 < ROPE_HEADS:
-                    dst, col = out_1, (head0 - Q_HEADS) * P
-                else:
-                    dst, col = out_2, (head0 - ROPE_HEADS) * P
-                nc.sync.dma_start(
-                    out=dst.rearrange("(b p) h d -> p b (h d)", p=P)[
-                        :, th * BLOCKS : (th + 1) * BLOCKS, col + lo : col + (a + 1) * P
-                    ],
-                    in_=stg[:, :, lo : (a + 1) * P],
-                )
-
-        def finish_both(unit0, unit1):
-            i, th, a0 = unit0
+        def finish_both(i, th, split_store):
             head0 = 2 * PAIR_ORDER[i]
             stg = work.tile([P, BLOCKS, 2 * P], F32, tag="stg", name="stg", bufs=STG_BUFS)
             ots = []
-            for unit in (unit0, unit1):
+            for a in range(2):
                 ot = psum.tile([P, BLOCKS, P], F32, tag="bank", name="ot", bufs=BANKS)
                 ots.append(ot)
             for b in range(BLOCKS):
                 cols = slice(b * P, (b + 1) * P)
-                for ot, unit in zip(ots, (unit0, unit1)):
+                for a in range(2):
                     nc.tensor.matmul(
-                        ot[:, b, :], lhsT=terms[unit][:, 0, cols], rhs=ident[:], is_transpose=True, start=True, stop=False
+                        ots[a][:, b, :], lhsT=terms[(i, th, a)][:, 0, cols], rhs=ident[:], is_transpose=True,
+                        start=True, stop=False,
                     )
-                for ot, unit in zip(ots, (unit0, unit1)):
+                for a in range(2):
                     nc.tensor.matmul(
-                        ot[:, b, :], lhsT=terms[unit][:, 1, cols], rhs=swap[:], is_transpose=True, start=False, stop=True
+                        ots[a][:, b, :], lhsT=terms[(i, th, a)][:, 1, cols], rhs=swap[:], is_transpose=True,
+                        start=False, stop=True,
                     )
             if head0 < Q_HEADS:
                 dst, col = out_0, head0 * P
             else:
                 dst, col = out_1, (head0 - Q_HEADS) * P
-            at_end = i == PAIRS - 1 and th == TOK_HALVES - 1
-            for a, ot in enumerate(ots):
-                nc.scalar.copy(out=stg[:, :, a * P : (a + 1) * P], in_=ot[:])
-                if a == 1 or at_end:
-                    lo = a * P if at_end else 0
+            for a in range(2):
+                nc.scalar.copy(out=stg[:, :, a * P : (a + 1) * P], in_=ots[a][:])
+                if a == 1 or split_store:
+                    lo = a * P if split_store else 0
                     nc.sync.dma_start(
                         out=dst.rearrange("(b p) h d -> p b (h d)", p=P)[
                             :, th * BLOCKS : (th + 1) * BLOCKS, col + lo : col + (a + 1) * P
@@ -332,24 +278,55 @@ def tile_flashqwen2attention_pa_kernel(
                         in_=stg[:, :, lo : (a + 1) * P],
                     )
 
+        vacc = {}
+
+        def multiply_value(t):
+            toks = slice(t * P, (t + 1) * P)
+            chans = slice(ROPE_HEADS * P, HEADS * P)
+            bank = psum.tile([P, VALUE_PAIRS * 2 * P], F32, tag="bank", name="vacc", bufs=BANKS)
+            for g in range(PASSES):
+                nc.tensor.matmul_mx(
+                    out=bank[:],
+                    lhsT=h_codes[:, g, toks].bitcast(FP8X4),
+                    lhsT_scale=h_scales[:, g, toks],
+                    rhs=w_codes[:, g, chans].bitcast(FP8X4),
+                    rhs_scale=w_scales[:, g, chans],
+                    start=(g == 0),
+                    stop=(g == PASSES - 1),
+                )
+            vacc[t] = bank
+
+        def store_value(t):
+            vo = work.tile([P, VALUE_PAIRS * 2 * P], F32, tag="uv", name="vo", bufs=UV_BUFS)
+            nc.vector.tensor_tensor(out=vo[:], in0=vacc[t][:], in1=bias_row[:], op=ALU.add)
+            nc.sync.dma_start(out=out_2.rearrange("(t p) h d -> p t (h d)", p=P)[:, t, :], in_=vo[:])
+
         def bias_table():
             bt = psum.tile([P, P], BF16, tag="bank", name="bt", bufs=BANKS)
             nc.tensor.transpose(bt[:], b_rows[:], ident_bf[:])
             nc.vector.tensor_copy(out=bias_col[:], in_=bt[:, 0:HEADS])
+
+        def value_bias():
+            vb = psum.tile([P, VALUE_PAIRS * 2, P], F32, tag="bank", name="vb", bufs=BANKS)
+            for c in range(VALUE_PAIRS * 2):
+                head = ROPE_HEADS + c
+                nc.tensor.transpose(vb[:, c, :], bias_col[:, head : head + 1].to_broadcast([P, P]), ident[:])
+            nc.scalar.copy(out=bias_row[:], in_=vb[:].rearrange("p c n -> p (c n)"))
 
         def scale_columns():
             sc = psum.tile([P, P], F32, tag="bank", name="sc", bufs=BANKS)
             nc.tensor.transpose(sc[:], s_rows[:], ident[:])
             nc.vector.tensor_copy(out=scl_col[:], in_=sc[:, 0 : K // P])
 
-        def spread_scales(b):
+        def spread_scales(b, on_vector):
             st = psum.tile([P, BLOCKS, P], F32, tag="bank", name="st", bufs=BANKS)
             for c in range(BLOCKS):
                 col = BLOCKS * b + c
                 nc.tensor.transpose(st[:, c, :], scl_col[:, col : col + 1].to_broadcast([P, P]), ident[:])
-            nc.vector.tensor_copy(
-                out=scl[:, b * K_PASS : (b + 1) * K_PASS], in_=st[:].rearrange("p c n -> p (c n)")
-            )
+            if on_vector:
+                nc.vector.tensor_copy(out=scl[:, cols_of(b)], in_=st[:].rearrange("p c n -> p (c n)"))
+            else:
+                nc.scalar.copy(out=scl[:, cols_of(b)], in_=st[:].rearrange("p c n -> p (c n)"))
 
         def angle_tables():
             for which in range(2):
@@ -357,124 +334,132 @@ def tile_flashqwen2attention_pa_kernel(
                 for a in range(TOK_TILES):
                     nc.tensor.transpose(ct[:, a, :], cs_rows[:, which, a, :], ident_bf[:])
                 if which == 0:
-                    nc.scalar.copy(out=cs_t[:, 0, :], in_=ct[:].rearrange("p a t -> p (a t)"))
+                    nc.vector.tensor_copy(out=cs_t[:, 0, :], in_=ct[:].rearrange("p a t -> p (a t)"))
                 else:
-                    nc.scalar.activation(
-                        out=cs_t[:, 1, :], in_=ct[:].rearrange("p a t -> p (a t)"), func=ACT.Copy,
-                        scale=sgn[:, 0:1],
+                    nc.vector.tensor_scalar(
+                        out=cs_t[:, 1, :], in0=ct[:].rearrange("p a t -> p (a t)"), scalar1=sgn[:, 0:1],
+                        scalar2=None, op0=ALU.mult,
                     )
 
-        scale_columns()
-        for g in range(PASSES):
-            spread_scales(g)
-            for a in range(2):
-                widen(0, a, g * K_PASS, (g + 1) * K_PASS)
-        head_keys = [("h", 0, g) for g in range(PASSES)]
-        head_keys += [("w", 0, g) for g in range(PASSES)]
-        head_keys += [("h", 1, g) for g in range(PASSES)]
-        head_tags = ["ot", "ot", "acc", "acc", "acc", "tw", "tw", "tw", "ot"]
-        for key, tag in zip(head_keys, head_tags):
-            turn(key, tag)
-        for key in head_keys:
-            quantize(key)
-        bias_table()
+        def gp_parts(j):
+            return [(j, 0, g) for g in range(PASSES)]
 
-        units = [(i, th, a) for i in range(PAIRS) for th in range(TOK_HALVES) for a in range(2)]
-        banks = [("h", 2, g) for g in range(PASSES)] + [("h", 3, g) for g in range(PASSES)]
-        banks += [("w", 1, g) for g in range(PASSES)] + ["tables"]
-        banks += [("w", i, g) for i in range(2, PAIRS) for g in range(PASSES)]
-        heads_to_widen = [(i, a) for i in range(1, GP_FIRST) for a in range(2)]
+        def vec_parts(j):
+            return [(j, 1, g) for g in range(PASSES)]
 
-        def banks_in_step(s):
-            if s < 3:
-                return (6, 3, 2)[s]
-            if s < EARLY:
-                return 1
-            return 1 if s % 4 != SKIP else 0
-
-        def widenings_in_step(s):
-            if s == 0:
-                return 2
-            if s < 8:
-                return 1
-            return 1 if (s - 8) % 5 in (0, 2) else 0
-
-        turn_step = {}
-        counted = 0
-        for s in range(len(units) + LAG):
-            for n in range(banks_in_step(s)):
-                if counted < len(banks):
-                    turn_step[banks[counted]] = s
-                    counted += 1
-        gp_parts = {}
-        vec_parts = {}
-        sort_parts = {}
-        gp_step = GP_START
-        for i in range(GP_FIRST, PAIRS):
+        def turn_pair(j):
             for g in range(PASSES):
-                due = turn_step[("w", i, g)]
-                if gp_step + 1 + GP_MARGIN <= due:
-                    gp_parts[gp_step] = (i, 0, g)
-                    gp_parts[gp_step + 1] = (i, 1, g)
-                    gp_step += 2
-                else:
-                    for a in range(2):
-                        vec_parts[due - VEC_AHEAD + a] = (i, a, g)
-                        sort_parts[due - VEC_AHEAD + a + PART_SORT_LAG] = (i, a, g)
+                turn(("w", j, g))
 
-        emptied = []
-        widened = []
-        next_head = 0
-        next_bank = 0
-        steps = len(units) + LAG
-        starts = list(range(0, BIG_FROM, GROUP)) + list(range(BIG_FROM, steps, BIG))
-        for s0, s1 in zip(starts, starts[1:] + [steps]):
-            group = range(s0, s1)
-            if s0 < BIG_FROM:
-                for key in emptied:
-                    quantize(key)
-                emptied = []
-            for s in group:
-                if s < len(units):
-                    multiply(units[s])
-                    rotate(units[s])
-            for key in emptied:
-                quantize(key)
-            emptied = []
-            for s in group:
-                for i, a in widened[s - SORT_LAG] if s >= SORT_LAG else []:
-                    sort_words(i, a)
-                if s in gp_parts:
-                    i, a, g = gp_parts[s]
-                    cast_part(i, a, g)
-                    scale_part(i, a, g)
-                if s in sort_parts:
-                    i, a, g = sort_parts[s]
-                    sort_part(i, a, g)
-                if s in vec_parts:
-                    i, a, g = vec_parts[s]
-                    widen_part(i, a, g)
-                widened.append([])
-                for n in range(widenings_in_step(s)):
-                    if next_head < len(heads_to_widen):
-                        i, a = heads_to_widen[next_head]
-                        next_head += 1
-                        widen(i, a, 0, K)
-                        if i >= FIRST_SORTED:
-                            widened[s].append((i, a))
-            for s in group:
-                if LAG <= s < len(units) + LAG:
-                    if 2 * PAIR_ORDER[units[s - LAG][0]] >= ROPE_HEADS or s - LAG >= len(units) - 2:
-                        finish(units[s - LAG])
-                    elif units[s - LAG][2] == 0:
-                        finish_both(units[s - LAG], units[s - LAG + 1])
-            for s in group:
-                for n in range(banks_in_step(s)):
-                    if next_bank < len(banks):
-                        key = banks[next_bank]
-                        next_bank += 1
-                        if key == "tables":
-                            angle_tables()
-                        else:
-                            turn(key, "tw")
-                            emptied.append(key)
+        def quantize_pair(j):
+            for g in range(PASSES):
+                quantize(("w", j, g))
+
+        def cast_and_scale(parts):
+            for p3 in parts:
+                cast_part(*p3)
+                scale_part(*p3)
+
+        scale_columns()
+        bias_table()
+        spread_scales(0, True)
+        spread_scales(1, False)
+        spread_scales(2, False)
+        for g in range(PASSES):
+            for a in range(2):
+                widen_plain(0, a, g)
+        h0 = [("h", 0, g) for g in range(PASSES)]
+        h1 = [("h", 1, g) for g in range(PASSES)]
+        for key in h0:
+            open_bank(key)
+        for a in range(2):
+            for key in h0:
+                turn_rows(key, a)
+        for key in h0:
+            empty(key)
+        turn(("w", 0, 0))
+        for key in h1:
+            open_bank(key)
+        for key in h1:
+            turn_rows(key, 0)
+        turn(("w", 0, 1))
+        for key in h1:
+            turn_rows(key, 1)
+        for key in h1:
+            empty(key)
+        turn(("w", 0, 2))
+        for key in h0:
+            quantize(key)
+        quantize(("w", 0, 0))
+        widen_plain(1, 1, 0)
+        quantize(("w", 0, 1))
+        widen_plain(1, 1, 1)
+        for key in h1:
+            quantize(key)
+        quantize(("w", 0, 2))
+        widen_plain(1, 1, 2)
+        angle_tables()
+        for p3 in gp_parts(1)[0:2]:
+            cast_part(*p3)
+
+        for a in range(2):
+            multiply((0, 0, a))
+            rotate((0, 0, a))
+        for p3 in gp_parts(1)[0:2]:
+            scale_part(*p3)
+        h2 = [("h", 2, g) for g in range(PASSES)]
+        h3 = [("h", 3, g) for g in range(PASSES)]
+        for key in h2 + h3:
+            turn(key)
+        widen_plain(1, 0, 2)
+        for key in h2:
+            quantize(key)
+        widen_part(2, 1, 0)
+        for key in h3:
+            quantize(key)
+        widen_part(2, 1, 1)
+        for g in range(PASSES):
+            turn(("w", 1, g))
+        finish_both(0, 0, False)
+        for g in range(PASSES):
+            quantize(("w", 1, g))
+        widen_part(2, 1, 2)
+        for a in range(2):
+            multiply((0, 1, a))
+            rotate((0, 1, a))
+        cast_and_scale(gp_parts(2))
+        for p3 in vec_parts(2):
+            sort_part(*p3)
+        cast_and_scale(gp_parts(3))
+
+        for j in range(1, ROPE_PAIRS):
+            last = j == ROPE_PAIRS - 1
+            for th in range(TOK_HALVES):
+                for a in range(2):
+                    multiply((j, th, a))
+                    rotate((j, th, a))
+            turn_pair(j + 1)
+            quantize_pair(j + 1)
+            if last:
+                turn_pair(j + 2)
+                quantize_pair(j + 2)
+            else:
+                ahead = [j + 2, j + 3] if j + 3 == PAIRS - 1 else [j + 2]
+                for n in ahead:
+                    for p3 in vec_parts(n):
+                        widen_part(*p3)
+            finish_both(j - 1, 1, False)
+            finish_both(j, 0, False)
+            if j == 4:
+                value_bias()
+            if not last:
+                if j + 3 < PAIRS:
+                    cast_and_scale(gp_parts(j + 3))
+                for n in ahead:
+                    for p3 in vec_parts(n):
+                        sort_part(*p3)
+
+        finish_both(ROPE_PAIRS - 1, 1, False)
+        for t in range(TOK_TILES):
+            multiply_value(t)
+            store_value(t)

@@ -34,7 +34,7 @@ ROPE_PAIRS = 8
 
 BANKS = 8
 UV_BUFS = 8
-STG_BUFS = 4
+STG_BUFS = 3
 RAW_BUFS = 10
 WS_BUFS = 20
 GRP_BUFS = 9
@@ -244,9 +244,14 @@ def tile_flashqwen2attention_pa_kernel(
             )
             terms[unit] = uv
 
+        staged = {}
+
         def finish_both(i, th, split_store):
             head0 = 2 * PAIR_ORDER[i]
-            stg = work.tile([P, BLOCKS, 2 * P], F32, tag="stg", name="stg", bufs=STG_BUFS)
+            if th == 0:
+                stg = work.tile([P, TOK_TILES, 2 * P], F32, tag="stg", name="stg", bufs=STG_BUFS)
+                staged[i] = stg
+            stg = staged[i]
             ots = []
             for a in range(2):
                 ot = psum.tile([P, BLOCKS, P], F32, tag="bank", name="ot", bufs=BANKS)
@@ -268,15 +273,11 @@ def tile_flashqwen2attention_pa_kernel(
             else:
                 dst, col = out_1, (head0 - Q_HEADS) * P
             for a in range(2):
-                nc.scalar.copy(out=stg[:, :, a * P : (a + 1) * P], in_=ots[a][:])
-                if a == 1 or split_store:
-                    lo = a * P if split_store else 0
-                    nc.sync.dma_start(
-                        out=dst.rearrange("(b p) h d -> p b (h d)", p=P)[
-                            :, th * BLOCKS : (th + 1) * BLOCKS, col + lo : col + (a + 1) * P
-                        ],
-                        in_=stg[:, :, lo : (a + 1) * P],
-                    )
+                nc.scalar.copy(out=stg[:, th * BLOCKS : (th + 1) * BLOCKS, a * P : (a + 1) * P], in_=ots[a][:])
+            if th == TOK_HALVES - 1:
+                nc.sync.dma_start(
+                    out=dst.rearrange("(b p) h d -> p b (h d)", p=P)[:, :, col : col + 2 * P], in_=stg[:]
+                )
 
         vacc = {}
 

@@ -75,17 +75,13 @@ def tile_flashqwen2attention_pa_kernel(
         b_rows = const.tile([P, P], BF16, name="b_rows")
         nc.gpsimd.memset(b_rows[:], 0.0)
         nc.sync.dma_start(out=b_rows[0:HEADS, :], in_=qkv_b.rearrange("(h p) -> h p", p=P))
+        cs_raw = const.tile([P, 2, TOK_TILES * HALF], BF16, name="cs_raw")
+        for which, table in enumerate((cos, sin)):
+            nc.sync.dma_start(out=cs_raw[:, which, :], in_=table.rearrange("(p a) j -> p (a j)", a=TOK_TILES))
         load_w(0)
         for a in range(0, 4):
             load_hid(a)
         load_w(1)
-        cs_rows = const.tile([P, 2, TOK_TILES, P], BF16, name="cs_rows")
-        for which, table in enumerate((cos, sin)):
-            for half in range(2):
-                nc.sync.dma_start(
-                    out=cs_rows[:, which, :, half * HALF : (half + 1) * HALF],
-                    in_=table.rearrange("(a p) j -> p a j", p=P),
-                )
         load_w(2)
         for a in range(4, 8):
             load_hid(a)
@@ -110,6 +106,7 @@ def tile_flashqwen2attention_pa_kernel(
         bias_col = const.tile([P, HEADS], F32, name="bias_col")
         bias_row = const.tile([P, VALUE_PAIRS * 2 * P], F32, name="bias_row")
         cs_t = const.tile([P, 2, T], BF16, name="cs_t")
+        cs_rows = const.tile([P, 2, TOK_TILES, 2, HALF], BF16, name="cs_rows")
 
         w_codes = const.tile([P, PASSES, HEADS * P], U32, name="w_codes", align_bytes=64)
         w_scales = const.tile([P, PASSES, HEADS * P], U8, name="w_scales", align_bytes=64)
@@ -329,17 +326,29 @@ def tile_flashqwen2attention_pa_kernel(
             else:
                 nc.scalar.copy(out=scl[:, cols_of(b)], in_=st[:].rearrange("p c n -> p (c n)"))
 
+        def double_angles():
+            nc.scalar.copy(
+                out=cs_rows[:].rearrange("p w a d j -> p (w a) d j"),
+                in_=cs_raw[:].rearrange("p w (a j) -> p (w a) j", j=HALF).unsqueeze(2).to_broadcast(
+                    [P, 2 * TOK_TILES, 2, HALF]
+                ),
+            )
+
         def angle_tables():
             for which in range(2):
                 ct = psum.tile([P, TOK_TILES, P], BF16, tag="bank", name="ct", bufs=BANKS)
                 for a in range(TOK_TILES):
-                    nc.tensor.transpose(ct[:, a, :], cs_rows[:, which, a, :], ident_bf[:])
+                    nc.tensor.transpose(
+                        ct[:, a, :], cs_rows[:, which, a, :, :].rearrange("p d j -> p (d j)"), ident_bf[:]
+                    )
                 if which == 0:
-                    nc.vector.tensor_copy(out=cs_t[:, 0, :], in_=ct[:].rearrange("p a t -> p (a t)"))
+                    nc.vector.tensor_copy(
+                        out=cs_t[:, 0, :].rearrange("c (p a) -> c p a", a=TOK_TILES), in_=ct[:].rearrange("c a p -> c p a")
+                    )
                 else:
                     nc.vector.tensor_scalar(
-                        out=cs_t[:, 1, :], in0=ct[:].rearrange("p a t -> p (a t)"), scalar1=sgn[:, 0:1],
-                        scalar2=None, op0=ALU.mult,
+                        out=cs_t[:, 1, :].rearrange("c (p a) -> c p a", a=TOK_TILES), in0=ct[:].rearrange("c a p -> c p a"),
+                        scalar1=sgn[:, 0:1], scalar2=None, op0=ALU.mult,
                     )
 
         def gp_parts(j):
@@ -366,6 +375,7 @@ def tile_flashqwen2attention_pa_kernel(
         spread_scales(0, True)
         spread_scales(1, False)
         spread_scales(2, False)
+        double_angles()
         for g in range(PASSES):
             for a in range(2):
                 widen_plain(0, a, g)

@@ -82,10 +82,9 @@ def tile_flashqwen2attention_pa_kernel(
         for a in range(0, 4):
             load_hid(a)
         load_w(1)
-        load_w(2)
         for a in range(4, 8):
             load_hid(a)
-        for i in range(3, PAIRS):
+        for i in range(2, PAIRS):
             load_w(i)
 
         ident = const.tile([P, P], F32, name="ident")
@@ -271,10 +270,12 @@ def tile_flashqwen2attention_pa_kernel(
                 dst, col = out_1, (head0 - Q_HEADS) * P
             for a in range(2):
                 nc.scalar.copy(out=stg[:, th * BLOCKS : (th + 1) * BLOCKS, a * P : (a + 1) * P], in_=ots[a][:])
-            if th == TOK_HALVES - 1:
-                nc.sync.dma_start(
-                    out=dst.rearrange("(b p) h d -> p b (h d)", p=P)[:, :, col : col + 2 * P], in_=stg[:]
-                )
+            view = dst.rearrange("(b p) h d -> p b (h d)", p=P)
+            if split_store:
+                blocks = slice(th * BLOCKS, (th + 1) * BLOCKS)
+                nc.sync.dma_start(out=view[:, blocks, col : col + 2 * P], in_=stg[:, blocks, :])
+            elif th == TOK_HALVES - 1:
+                nc.sync.dma_start(out=view[:, :, col : col + 2 * P], in_=stg[:])
 
         vacc = {}
 
@@ -431,7 +432,7 @@ def tile_flashqwen2attention_pa_kernel(
         widen_part(2, 1, 1)
         for g in range(PASSES):
             turn(("w", 1, g))
-        finish_both(0, 0, False)
+        finish_both(0, 0, True)
         for g in range(PASSES):
             quantize(("w", 1, g))
         widen_part(2, 1, 2)
@@ -449,6 +450,8 @@ def tile_flashqwen2attention_pa_kernel(
                 for a in range(2):
                     multiply((j, th, a))
                     rotate((j, th, a))
+            if last:
+                finish_both(j - 1, 1, True)
             turn_pair(j + 1)
             quantize_pair(j + 1)
             if last:
@@ -459,8 +462,9 @@ def tile_flashqwen2attention_pa_kernel(
                 for n in ahead:
                     for p3 in vec_parts(n):
                         widen_part(*p3)
-            finish_both(j - 1, 1, False)
-            finish_both(j, 0, False)
+            if not last:
+                finish_both(j - 1, 1, True)
+            finish_both(j, 0, True)
             if j == 4:
                 value_bias()
             if not last:
@@ -470,7 +474,7 @@ def tile_flashqwen2attention_pa_kernel(
                     for p3 in vec_parts(n):
                         sort_part(*p3)
 
-        finish_both(ROPE_PAIRS - 1, 1, False)
+        finish_both(ROPE_PAIRS - 1, 1, True)
         for t in range(TOK_TILES):
             multiply_value(t)
             store_value(t)

from contextlib import ExitStack

import concourse.masks as masks
import concourse.mybir as mybir

F32 = mybir.dt.float32
BF16 = mybir.dt.bfloat16
U32 = mybir.dt.uint32
U8 = mybir.dt.uint8
FP8 = mybir.dt.float8_e4m3fn
FP8X4 = mybir.dt.float8_e4m3fn_x4
ALU = mybir.AluOpType
ACT = mybir.ActivationFunctionType

P = 128
T = 1024
K = 1536
HEADS = 20
Q_HEADS = 12
ROPE_HEADS = 16
HALF = 64
K_PASS = 512
PASSES = K // K_PASS
WORDS = K_PASS // 2
TOK_TILES = T // P
N_TOK = 512
TOK_HALVES = T // N_TOK
BLOCKS = N_TOK // P
PAIRS = HEADS // 2
VALUE_PAIRS = 2

PAIR_ORDER = [0, 1, 2, 3, 4, 5, 6, 7, 8, 9]
ROPE_PAIRS = 8

BANKS = 8
UV_BUFS = 8
STG_BUFS = 3
RAW_BUFS = 10
WS_BUFS = 20
GRP_BUFS = 9

FLOPS = 2 * T * K * HEADS * P


def tile_flashqwen2attention_pa_kernel(
    tc, hidden_states, cos, sin, qkv_w_bytes, qkv_w_scale, qkv_b, out_0, out_1, out_2
):
    nc = tc.nc

    with ExitStack() as ctx:
        const = ctx.enter_context(tc.tile_pool(name="const", bufs=1))
        work = ctx.enter_context(tc.tile_pool(name="work", bufs=2))
        psum = ctx.enter_context(tc.psum_pool(name="psum", bufs=2))
        ctx.enter_context(tc.manual_schedule())

        w_view = qkv_w_bytes.rearrange("(h p) k -> p h k", p=P)
        hid_view = hidden_states.rearrange("(a p) k -> p a k", p=P)
        w_bytes = {}
        hid = {}

        def load_w(i):
            pair = PAIR_ORDER[i]
            t = const.tile([P, 2, K], U8, name="w_bytes_%d" % i)
            nc.sync.dma_start(out=t[:], in_=w_view[:, 2 * pair : 2 * pair + 2, :])
            w_bytes[i] = t

        def load_hid(a):
            t = const.tile([P, K], BF16, name="hid_%d" % a)
            nc.sync.dma_start(out=t[:], in_=hid_view[:, a, :])
            hid[a] = t

        s_rows = const.tile([P, P], F32, name="s_rows")
        nc.gpsimd.memset(s_rows[:], 0.0)
        nc.sync.dma_start(out=s_rows[0 : K // P, :], in_=qkv_w_scale.rearrange("o (c p) -> (o c) p", p=P))
        b_rows = const.tile([P, P], BF16, name="b_rows")
        nc.gpsimd.memset(b_rows[:], 0.0)
        nc.sync.dma_start(out=b_rows[0:HEADS, :], in_=qkv_b.rearrange("(h p) -> h p", p=P))
        cs_raw = const.tile([P, 2, TOK_TILES * HALF], BF16, name="cs_raw")
        for which, table in enumerate((cos, sin)):
            nc.sync.dma_start(out=cs_raw[:, which, :], in_=table.rearrange("(p a) j -> p (a j)", a=TOK_TILES))
        load_w(0)
        for a in range(0, 4):
            load_hid(a)
        load_w(1)
        for a in range(4, 8):
            load_hid(a)
        for i in range(2, PAIRS):
            load_w(i)

        ident = const.tile([P, P], F32, name="ident")
        masks.make_identity(nc, ident[:])
        ident_bf = const.tile([P, P], BF16, name="ident_bf")
        masks.make_identity(nc, ident_bf[:])
        swap = const.tile([P, P], F32, name="swap")
        nc.vector.tensor_copy(out=swap[:, 0:HALF], in_=ident[:, HALF:P])
        nc.vector.tensor_copy(out=swap[:, HALF:P], in_=ident[:, 0:HALF])
        sgn = const.tile([P, 1], F32, name="sgn")
        nc.vector.memset(sgn[0:HALF, :], 1.0)
        nc.vector.memset(sgn[HALF:P, :], -1.0)
        warm = const.tile([P, 1], F32, name="warm")
        nc.scalar.activation(out=warm[:], in_=sgn[:], func=ACT.Identity)

        scl_col = const.tile([P, K // P], F32, name="scl_col")
        scl = const.tile([P, K], F32, name="scl")
        bias_col = const.tile([P, HEADS], F32, name="bias_col")
        bias_row = const.tile([P, VALUE_PAIRS * 2 * P], F32, name="bias_row")
        cs_t = const.tile([P, 2, T], BF16, name="cs_t")
        cs_rows = const.tile([P, 2, TOK_TILES, 2, HALF], BF16, name="cs_rows")

        w_codes = const.tile([P, PASSES, HEADS * P], U32, name="w_codes", align_bytes=64)
        w_scales = const.tile([P, PASSES, HEADS * P], U8, name="w_scales", align_bytes=64)
        h_codes = const.tile([P, PASSES, T], U32, name="h_codes", align_bytes=64)
        h_scales = const.tile([P, PASSES, T], U8, name="h_scales", align_bytes=64)

        raw = {}
        part = {}
        is_sorted = {}
        grouped = {}

        def cols_of(g):
            return slice(g * K_PASS, (g + 1) * K_PASS)

        def widen_plain(i, a, g):
            t = work.tile([P, K_PASS], BF16, tag="ws", name="ws", bufs=WS_BUFS)
            nc.vector.tensor_tensor(
                out=t[:], in0=w_bytes[i][:, a, cols_of(g)].bitcast(FP8), in1=scl[:, cols_of(g)], op=ALU.mult
            )
            part[(i, a, g)] = t
            is_sorted[(i, a, g)] = False

        def widen_part(i, a, g):
            t = work.tile([P, K_PASS], BF16, tag="raw", name="raw", bufs=RAW_BUFS)
            nc.vector.tensor_tensor(
                out=t[:], in0=w_bytes[i][:, a, cols_of(g)].bitcast(FP8), in1=scl[:, cols_of(g)], op=ALU.mult
            )
            raw[(i, a, g)] = t

        def sort_part(i, a, g):
            t = work.tile([P, K_PASS], BF16, tag="ws", name="ws", bufs=WS_BUFS)
            nc.scalar.copy(
                out=t[:].bitcast(F32).rearrange("p (u w) -> p u w", u=2),
                in_=raw[(i, a, g)][:].bitcast(F32).rearrange("p (w u) -> p u w", u=2),
            )
            part[(i, a, g)] = t
            is_sorted[(i, a, g)] = True

        def cast_part(i, a, g):
            t = work.tile([P, K_PASS], BF16, tag="raw", name="raw", bufs=RAW_BUFS)
            nc.scalar.copy(out=t[:], in_=w_bytes[i][:, a, cols_of(g)].bitcast(FP8))
            raw[(i, a, g)] = t

        def scale_part(i, a, g):
            t = work.tile([P, K_PASS], BF16, tag="ws", name="ws", bufs=WS_BUFS)
            nc.gpsimd.tensor_tensor(
                out=t[:].rearrange("p (u w e) -> p u w e", u=2, e=2),
                in0=raw[(i, a, g)][:].rearrange("p (w u e) -> p u w e", u=2, e=2),
                in1=scl[:, cols_of(g)].rearrange("p (w u e) -> p u w e", u=2, e=2),
                op=ALU.mult,
            )
            part[(i, a, g)] = t
            is_sorted[(i, a, g)] = True

        turned = {}

        def open_bank(key):
            tw = psum.tile([P, 2, 2, P], F32, tag="bank", name="tw", bufs=BANKS)
            turned[key] = tw

        def turn_rows(key, a):
            kind, i, g = key
            for u in range(2):
                if kind == "h":
                    picked = hid[2 * i + a][:].bitcast(F32)[:, WORDS * g + u : WORDS * (g + 1) : 2]
                elif is_sorted[(i, a, g)]:
                    picked = part[(i, a, g)][:].bitcast(F32)[:, P * u : P * (u + 1)]
                else:
                    picked = part[(i, a, g)][:].bitcast(F32)[:, u:WORDS:2]
                nc.tensor.transpose(turned[key][:, a, u, :], picked, ident[:])

        def turn(key, on_vector=False):
            open_bank(key)
            for a in range(2):
                turn_rows(key, a)
            empty(key, on_vector)

        def empty(key, on_vector=False):
            tw = turned[key]
            grp = work.tile([P, 2 * P * 4], BF16, tag="grp", name="grp", bufs=GRP_BUFS, align_bytes=64)
            if on_vector:
                nc.vector.tensor_copy(
                    out=grp[:].bitcast(F32).rearrange("p (a r u) -> p a r u", a=2, u=2),
                    in_=tw[:].rearrange("p a u r -> p a r u"),
                )
            else:
                nc.scalar.copy(
                    out=grp[:].bitcast(F32).rearrange("p (a r u) -> p a r u", a=2, u=2),
                    in_=tw[:].rearrange("p a u r -> p a r u"),
                )
            grouped[key] = grp

        def quantize(key):
            kind, i, g = key
            codes, scales = (w_codes, w_scales) if kind == "w" else (h_codes, h_scales)
            cols = slice(2 * i * P, 2 * (i + 1) * P)
            nc.vector.quantize_mx(
                out=codes[:, g, cols].bitcast(FP8X4), scales=scales[:, g, cols], in_=grouped[key][:]
            )

        acc = {}
        terms = {}

        def multiply(unit):
            i, th, a = unit
            cols = slice((2 * i + a) * P, (2 * i + a + 1) * P)
            toks = slice(th * N_TOK, (th + 1) * N_TOK)
            bank = psum.tile([P, N_TOK], F32, tag="bank", name="acc", bufs=BANKS)
            for g in range(PASSES):
                nc.tensor.matmul_mx(
                    out=bank[:],
                    lhsT=w_codes[:, g, cols].bitcast(FP8X4),
                    lhsT_scale=w_scales[:, g, cols],
                    rhs=h_codes[:, g, toks].bitcast(FP8X4),
                    rhs_scale=h_scales[:, g, toks],
                    start=(g == 0),
                    stop=(g == PASSES - 1),
                )
            acc[unit] = bank

        def rotate(unit):
            i, th, a = unit
            head = 2 * PAIR_ORDER[i] + a
            uv = work.tile([P, 2, N_TOK], F32, tag="uv", name="uv", bufs=UV_BUFS)
            nc.vector.scalar_tensor_tensor(
                out=uv[:],
                in0=acc[unit][:].unsqueeze(1).to_broadcast([P, 2, N_TOK]),
                scalar=bias_col[:, head : head + 1],
                in1=cs_t[:, :, th * N_TOK : (th + 1) * N_TOK],
                op0=ALU.add,
                op1=ALU.mult,
            )
            terms[unit] = uv

        staged = {}

        def finish_both(i, th, split_store):
            head0 = 2 * PAIR_ORDER[i]
            if th == 0:
                stg = work.tile([P, TOK_TILES, 2 * P], F32, tag="stg", name="stg", bufs=STG_BUFS)
                staged[i] = stg
            stg = staged[i]
            ots = []
            for a in range(2):
                ot = psum.tile([P, BLOCKS, P], F32, tag="bank", name="ot", bufs=BANKS)
                ots.append(ot)
            for b in range(BLOCKS):
                cols = slice(b * P, (b + 1) * P)
                for a in range(2):
                    nc.tensor.matmul(
                        ots[a][:, b, :], lhsT=terms[(i, th, a)][:, 0, cols], rhs=ident[:], is_transpose=True,
                        start=True, stop=False,
                    )
                for a in range(2):
                    nc.tensor.matmul(
                        ots[a][:, b, :], lhsT=terms[(i, th, a)][:, 1, cols], rhs=swap[:], is_transpose=True,
                        start=False, stop=True,
                    )
            if head0 < Q_HEADS:
                dst, col = out_0, head0 * P
            else:
                dst, col = out_1, (head0 - Q_HEADS) * P
            for a in range(2):
                nc.scalar.copy(out=stg[:, th * BLOCKS : (th + 1) * BLOCKS, a * P : (a + 1) * P], in_=ots[a][:])
            view = dst.rearrange("(b p) h d -> p b (h d)", p=P)
            if split_store:
                blocks = slice(th * BLOCKS, (th + 1) * BLOCKS)
                nc.sync.dma_start(out=view[:, blocks, col : col + 2 * P], in_=stg[:, blocks, :])
            elif th == TOK_HALVES - 1:
                nc.sync.dma_start(out=view[:, :, col : col + 2 * P], in_=stg[:])

        vacc = {}

        def multiply_value(t):
            toks = slice(t * P, (t + 1) * P)
            chans = slice(ROPE_HEADS * P, HEADS * P)
            bank = psum.tile([P, VALUE_PAIRS * 2 * P], F32, tag="bank", name="vacc", bufs=BANKS)
            for g in range(PASSES):
                nc.tensor.matmul_mx(
                    out=bank[:],
                    lhsT=h_codes[:, g, toks].bitcast(FP8X4),
                    lhsT_scale=h_scales[:, g, toks],
                    rhs=w_codes[:, g, chans].bitcast(FP8X4),
                    rhs_scale=w_scales[:, g, chans],
                    start=(g == 0),
                    stop=(g == PASSES - 1),
                )
            vacc[t] = bank

        def store_value(t):
            vo = work.tile([P, VALUE_PAIRS * 2 * P], F32, tag="uv", name="vo", bufs=UV_BUFS)
            nc.vector.tensor_tensor(out=vo[:], in0=vacc[t][:], in1=bias_row[:], op=ALU.add)
            nc.sync.dma_start(out=out_2.rearrange("(t p) h d -> p t (h d)", p=P)[:, t, :], in_=vo[:])

        def bias_table():
            bt = psum.tile([P, P], BF16, tag="bank", name="bt", bufs=BANKS)
            nc.tensor.transpose(bt[:], b_rows[:], ident_bf[:])
            nc.vector.tensor_copy(out=bias_col[:], in_=bt[:, 0:HEADS])

        def value_bias():
            vb = psum.tile([P, VALUE_PAIRS * 2, P], F32, tag="bank", name="vb", bufs=BANKS)
            for c in range(VALUE_PAIRS * 2):
                head = ROPE_HEADS + c
                nc.tensor.transpose(vb[:, c, :], bias_col[:, head : head + 1].to_broadcast([P, P]), ident[:])
            nc.scalar.copy(out=bias_row[:], in_=vb[:].rearrange("p c n -> p (c n)"))

        def scale_columns():
            sc = psum.tile([P, P], F32, tag="bank", name="sc", bufs=BANKS)
            nc.tensor.transpose(sc[:], s_rows[:], ident[:])
            nc.vector.tensor_copy(out=scl_col[:], in_=sc[:, 0 : K // P])

        def spread_scales(b, on_vector):
            st = psum.tile([P, BLOCKS, P], F32, tag="bank", name="st", bufs=BANKS)
            for c in range(BLOCKS):
                col = BLOCKS * b + c
                nc.tensor.transpose(st[:, c, :], scl_col[:, col : col + 1].to_broadcast([P, P]), ident[:])
            if on_vector:
                nc.vector.tensor_copy(out=scl[:, cols_of(b)], in_=st[:].rearrange("p c n -> p (c n)"))
            else:
                nc.scalar.copy(out=scl[:, cols_of(b)], in_=st[:].rearrange("p c n -> p (c n)"))

        def double_angles():
            nc.scalar.copy(
                out=cs_rows[:].rearrange("p w a d j -> p (w a) d j"),
                in_=cs_raw[:].rearrange("p w (a j) -> p (w a) j", j=HALF).unsqueeze(2).to_broadcast(
                    [P, 2 * TOK_TILES, 2, HALF]
                ),
            )

        def angle_tables():
            for which in range(2):
                ct = psum.tile([P, TOK_TILES, P], BF16, tag="bank", name="ct", bufs=BANKS)
                for a in range(TOK_TILES):
                    nc.tensor.transpose(
                        ct[:, a, :], cs_rows[:, which, a, :, :].rearrange("p d j -> p (d j)"), ident_bf[:]
                    )
                if which == 0:
                    nc.vector.tensor_copy(
                        out=cs_t[:, 0, :].rearrange("c (p a) -> c p a", a=TOK_TILES), in_=ct[:].rearrange("c a p -> c p a")
                    )
                else:
                    nc.vector.tensor_scalar(
                        out=cs_t[:, 1, :].rearrange("c (p a) -> c p a", a=TOK_TILES), in0=ct[:].rearrange("c a p -> c p a"),
                        scalar1=sgn[:, 0:1], scalar2=None, op0=ALU.mult,
                    )

        def gp_parts(j):
            return [(j, 0, g) for g in range(PASSES)]

        def vec_parts(j):
            return [(j, 1, g) for g in range(PASSES)]

        def turn_pair(j):
            for g in range(PASSES):
                turn(("w", j, g))

        def quantize_pair(j):
            for g in range(PASSES):
                quantize(("w", j, g))

        def cast_and_scale(parts):
            for p3 in parts:
                cast_part(*p3)
                scale_part(*p3)

        scale_columns()
        bias_table()
        spread_scales(0, True)
        spread_scales(1, False)
        spread_scales(2, False)
        double_angles()
        for g in range(PASSES):
            for a in range(2):
                widen_plain(0, a, g)
        h0 = [("h", 0, g) for g in range(PASSES)]
        h1 = [("h", 1, g) for g in range(PASSES)]
        for key in h0:
            open_bank(key)
        for a in range(2):
            for key in h0:
                turn_rows(key, a)
        for key in h0:
            empty(key)
        turn(("w", 0, 0))
        for key in h1:
            open_bank(key)
        for key in h1:
            turn_rows(key, 0)
        turn(("w", 0, 1))
        for key in h1:
            turn_rows(key, 1)
        for key in h1:
            empty(key)
        turn(("w", 0, 2))
        for key in h0:
            quantize(key)
        quantize(("w", 0, 0))
        widen_plain(1, 1, 0)
        quantize(("w", 0, 1))
        widen_plain(1, 1, 1)
        for key in h1:
            quantize(key)
        quantize(("w", 0, 2))
        widen_plain(1, 1, 2)
        angle_tables()
        for p3 in gp_parts(1)[0:2]:
            cast_part(*p3)

        for a in range(2):
            multiply((0, 0, a))
            rotate((0, 0, a))
        for p3 in gp_parts(1)[0:2]:
            scale_part(*p3)
        h2 = [("h", 2, g) for g in range(PASSES)]
        h3 = [("h", 3, g) for g in range(PASSES)]
        for key in h2 + h3:
            turn(key)
        widen_plain(1, 0, 2)
        for key in h2:
            quantize(key)
        widen_part(2, 1, 0)
        for key in h3:
            quantize(key)
        widen_part(2, 1, 1)
        for g in range(PASSES):
            turn(("w", 1, g))
        finish_both(0, 0, True)
        for g in range(PASSES):
            quantize(("w", 1, g))
        widen_part(2, 1, 2)
        for a in range(2):
            multiply((0, 1, a))
            rotate((0, 1, a))
        cast_and_scale(gp_parts(2))
        for p3 in vec_parts(2):
            sort_part(*p3)
        cast_and_scale(gp_parts(3))

        for j in range(1, ROPE_PAIRS):
            last = j == ROPE_PAIRS - 1
            for th in range(TOK_HALVES):
                for a in range(2):
                    multiply((j, th, a))
                    rotate((j, th, a))
            if last:
                finish_both(j - 1, 1, True)
            turn_pair(j + 1)
            quantize_pair(j + 1)
            if last:
                turn_pair(j + 2)
                quantize_pair(j + 2)
            else:
                ahead = [j + 2, j + 3] if j + 3 == PAIRS - 1 else [j + 2]
                for n in ahead:
                    for p3 in vec_parts(n):
                        widen_part(*p3)
            if not last:
                finish_both(j - 1, 1, True)
            finish_both(j, 0, True)
            if j == 4:
                value_bias()
            if not last:
                if j + 3 < PAIRS:
                    cast_and_scale(gp_parts(j + 3))
                for n in ahead:
                    for p3 in vec_parts(n):
                        sort_part(*p3)

        finish_both(ROPE_PAIRS - 1, 1, True)
        for t in range(TOK_TILES):
            multiply_value(t)
            store_value(t)
